import numpy as np
import ml_dtypes


def mxq(x, axis, fmt="e4m3"):
    dtype, down = {"e4m3": (ml_dtypes.float8_e4m3fn, 7), "e5m2": (ml_dtypes.float8_e5m2, 14)}[fmt]
    v = np.moveaxis(np.asarray(x, np.float32).astype(ml_dtypes.bfloat16).astype(np.float64), axis, -1)
    blocks = v.reshape(v.shape[:-1] + (-1, 32))
    amax = np.abs(blocks).max(-1, keepdims=True)
    byte = np.maximum(np.where(amax > 0, np.frexp(amax)[1] - 1 + 127, 0) - down, 1)
    scale = np.exp2(byte - 127.0)
    codes = (blocks / scale).astype(np.float32).astype(dtype).astype(np.float64)
    return np.moveaxis((codes * scale).reshape(v.shape), -1, axis)


WIDE = False


def mx_kscale(k):
    if not WIDE:
        return np.ones(k)
    levels = np.array([10, -10, 5, -5, 0])
    a = np.random.permutation(np.resize(levels, k // 512 * 4)).reshape(k // 512, 4)
    idx = np.arange(k)
    return np.exp2(a[idx // 512, idx % 128 // 32])


BF16 = ml_dtypes.bfloat16


def bf(x):
    return np.asarray(x, np.float32).astype(BF16)


def f64(x):
    return np.asarray(x).astype(np.float64)


E2M1 = np.array([0.0, 0.5, 1.0, 1.5, 2.0, 3.0, 4.0, 6.0, -0.0, -0.5, -1.0, -1.5, -2.0, -3.0, -4.0, -6.0])


def pack_weight(w, fmt):
    k, n = w.shape
    w = f64(bf(w)).reshape(k // 32, 32, n)
    amax = np.abs(w).max(1)
    if fmt == "e4m3":
        byte = np.frexp(amax)[1] - 1 + 127 - 7
    else:
        mant, ex = np.frexp(amax / 6.0)
        byte = np.where(mant > 0.5, ex, ex - 1) + 127
    byte = np.clip(np.where(amax > 0, byte, 1), 1, 254)
    scaled = (w * np.exp2(127.0 - byte)[:, None, :]).reshape(k, n).astype(np.float32)
    by_word = np.ascontiguousarray(scaled.reshape(k // 512, 128, 4, n).transpose(0, 1, 3, 2))
    if fmt == "e4m3":
        words = by_word.astype(ml_dtypes.float8_e4m3fn).view(np.uint8)
    else:
        c = by_word.astype(ml_dtypes.float4_e2m1fn).view(np.uint8) & 0xF
        words = c[..., 0::2] | (c[..., 1::2] << 4)
    return np.ascontiguousarray(words), np.ascontiguousarray(byte.astype(np.uint8).reshape(k // 512, 16, n))


def unpack_weight(words, scales, fmt):
    g, p, n, _ = words.shape
    if fmt == "e4m3":
        vals = np.ascontiguousarray(words).view(ml_dtypes.float8_e4m3fn).astype(np.float64)
    else:
        nib = np.empty((g, p, n, 4), np.uint8)
        nib[..., 0::2] = words & 0xF
        nib[..., 1::2] = words >> 4
        vals = E2M1[nib]
    vals = vals * np.repeat(np.exp2(scales.astype(np.float64) - 127.0), 8, axis=1)[..., None]
    return vals.transpose(0, 1, 3, 2).reshape(g * 512, n)


B, C, P, PB, D, H = 1, 1024, 4, 1, 1024, 2
R = D // H


def setup_inputs():
    t = np.tile(mx_kscale(R), H)[None, :, None]
    ws = 1.5 / np.sqrt(D)
    qz = bf(np.random.standard_normal((B, C, PB, D)))
    u = np.random.standard_normal((B, D, D)) * ws * t
    v = np.random.standard_normal((B, D, D)) * ws / t
    u_words, u_scales = pack_weight(u.swapaxes(1, 2).reshape(-1, D), "e4m3")
    v_words, v_scales = pack_weight(v.swapaxes(1, 2).reshape(-1, D), "e4m3")
    return {"qz": qz,
            "channel_u_w_words": u_words, "channel_u_w_scales": u_scales,
            "channel_v_w_words": v_words, "channel_v_w_scales": v_scales}


def reference(qz, channel_u_w_words, channel_u_w_scales, channel_v_w_words, channel_v_w_scales):
    x = f64(qz)
    xq = mxq(x, 3, "e4m3").reshape(B, C * PB, D)
    qu = xq @ unpack_weight(channel_u_w_words, channel_u_w_scales, "e4m3").reshape(B, D, D)
    qv = xq @ unpack_weight(channel_v_w_words, channel_v_w_scales, "e4m3").reshape(B, D, D)
    qu = qu.reshape(B, C, PB, H, R).transpose(0, 2, 3, 1, 4)
    qv = qv.reshape(B, C, PB, H, R).transpose(0, 2, 3, 1, 4)
    logits = (mxq(qu, 4, "e4m3") @ mxq(qv, 4, "e4m3").transpose(0, 1, 2, 4, 3)) * (1.0 / np.sqrt(R))
    e = np.exp(logits - logits.max(-1, keepdims=True))
    attn = e / e.sum(-1, keepdims=True)
    m = (attn * x.transpose(0, 2, 1, 3)[:, :, None, :, :]).mean(axis=2)
    return m.transpose(0, 2, 1, 3)

@@ -1,0 +1,241 @@
+import math
+
+import concourse.mybir as mybir
+from concourse.masks import make_identity
+
+F32 = mybir.dt.float32
+BF16 = mybir.dt.bfloat16
+I32 = mybir.dt.int32
+U32 = mybir.dt.uint32
+U8 = mybir.dt.uint8
+FP8X4 = mybir.dt.float8_e4m3fn_x4
+ALU = mybir.AluOpType
+ACT = mybir.ActivationFunctionType
+AXIS_X = mybir.AxisListType.X
+
+P = 128
+PACK = 4
+K_PASS = P * PACK
+C = 1024
+D = 1024
+HEADS = 2
+R = D // HEADS
+N_TILES = C // P
+G = D // K_PASS
+BANK = 512
+HALVES = C // BANK
+U_W = 0
+V_W = 1
+LOGIT_SCALE = 1.0 / math.sqrt(R)
+
+FLOPS = 2 * (2 * C * D * D) + HEADS * 2 * C * C * R
+
+
+def tile_dynamicptheadselection_pa_e_kernel(
+    tc, qz, u_words, u_scales, v_words, v_scales, out
+):
+    nc = tc.nc
+    x_dram = qz.rearrange("b c q d -> (b c q) d")
+    out_dram = out.rearrange("b c q d -> (b c q) d")
+    w_words_dram = [u_words, v_words]
+    w_scales_dram = [u_scales, v_scales]
+
+    with (
+        tc.tile_pool(name="keep", bufs=1) as keep,
+        tc.tile_pool(name="stage", bufs=4) as stage,
+        tc.tile_pool(name="rows", bufs=3) as rows,
+        tc.tile_pool(name="small", bufs=4) as small,
+        tc.psum_pool(name="psum_work", bufs=4) as psum_work,
+        tc.psum_pool(name="psum_logits", bufs=4) as psum_logits,
+    ):
+        x_sb = keep.tile([P, N_TILES, D], BF16)
+        x_codes = keep.tile([P, N_TILES, G * P], U32, align_bytes=64)
+        x_planes = keep.tile([P, N_TILES, G * P], U8, align_bytes=64)
+        w_codes = [
+            keep.tile([P, G, D], U32, align_bytes=64, name="w_codes_%d" % w) for w in (U_W, V_W)
+        ]
+        w_planes = keep.tile([P, D], U8, align_bytes=64)
+        q_codes = [
+            keep.tile([P, HEADS, C], U32, align_bytes=64, name="q_codes_%d" % w) for w in (U_W, V_W)
+        ]
+        q_planes = [
+            keep.tile([P, HEADS, C], U8, align_bytes=64, name="q_planes_%d" % w) for w in (U_W, V_W)
+        ]
+        share0 = keep.tile([P, N_TILES, C], F32)
+        sums = keep.tile([P, N_TILES, HEADS, HALVES], F32)
+        identity = keep.tile([P, P], F32)
+        warm = keep.tile([P, 1], F32)
+
+        nc.vector.memset(w_planes[:].bitcast(I32), 0)
+        nc.vector.memset(warm[:], 0.0)
+        nc.scalar.activation(out=warm[:], in_=warm[:], func=ACT.Exp)
+        make_identity(nc, identity[:])
+
+        def load_weight_codes(w, h):
+            cols = w_words_dram[w].rearrange("g p n t -> p g (n t)")
+            nc.sync.dma_start(
+                out=w_codes[w][:, :, R * h : R * (h + 1)].bitcast(I32),
+                in_=cols[:, :, PACK * R * h : PACK * R * (h + 1)].bitcast(I32),
+            )
+
+        def load_weight_scales(w):
+            for quadrant in range(4):
+                first = 32 * quadrant + PACK * G * w
+                nc.sync.dma_start(
+                    out=w_planes[first : first + PACK * G, :].bitcast(I32),
+                    in_=w_scales_dram[w][:, PACK * quadrant : PACK * (quadrant + 1), :].bitcast(I32),
+                )
+
+        for pair in range(N_TILES // 2):
+            nc.sync.dma_start(
+                out=x_sb[:, 2 * pair : 2 * pair + 2, :],
+                in_=x_dram[2 * P * pair : 2 * P * (pair + 1), :].rearrange("(i p) d -> p i d", p=P),
+            )
+        load_weight_scales(V_W)
+        load_weight_codes(V_W, 0)
+        load_weight_codes(U_W, 0)
+        load_weight_scales(U_W)
+        load_weight_codes(V_W, 1)
+        load_weight_codes(U_W, 1)
+
+        def copy_out(engine_is_scalar, dst, src):
+            if engine_is_scalar:
+                nc.scalar.copy(out=dst, in_=src)
+            else:
+                nc.vector.tensor_copy(out=dst, in_=src)
+
+        def quantise_x(i):
+            x_words = x_sb[:, i, :].bitcast(F32)
+            flipped = psum_work.tile([P, G, 2, P], F32, tag="work")
+            for g in range(G):
+                for u in range(2):
+                    nc.tensor.transpose(
+                        flipped[:, g, u, :],
+                        x_words[:, (K_PASS // 2) * g + u : (K_PASS // 2) * (g + 1) : 2],
+                        identity[:],
+                    )
+            x_grouped = stage.tile([P, G, P, PACK], BF16, align_bytes=64)
+            copy_out(
+                i % 2 == 0,
+                x_grouped[:].bitcast(F32),
+                flipped[:].rearrange("p g u c -> p g c u"),
+            )
+            nc.vector.quantize_mx(
+                out=x_codes[:, i, :].bitcast(FP8X4),
+                scales=x_planes[:, i, :],
+                in_=x_grouped[:].rearrange("p g c t -> p (g c t)"),
+            )
+
+        def project(w, h, i, on_scalar):
+            acc = psum_work.tile([P, PACK, P], F32, tag="work")
+            for t in range(PACK):
+                o_cols = slice(R * h + P * t, R * h + P * (t + 1))
+                for g in range(G):
+                    c_cols = slice(P * g, P * (g + 1))
+                    nc.tensor.matmul_mx(
+                        out=acc[:, t, :],
+                        lhsT=w_codes[w][:, g, o_cols].bitcast(FP8X4),
+                        lhsT_scale=w_planes[PACK * (G * w + g) : P, o_cols],
+                        rhs=x_codes[:, i, c_cols].bitcast(FP8X4),
+                        rhs_scale=x_planes[:, i, c_cols],
+                        start=(g == 0),
+                        stop=(g == G - 1),
+                    )
+            grouped = stage.tile([P, P, PACK], BF16, align_bytes=64)
+            copy_out(on_scalar, grouped[:], acc[:].rearrange("p t c -> p c t"))
+            channels = slice(P * i, P * (i + 1))
+            nc.vector.quantize_mx(
+                out=q_codes[w][:, h, channels].bitcast(FP8X4),
+                scales=q_planes[w][:, h, channels],
+                in_=grouped[:].rearrange("p c t -> p (c t)"),
+            )
+
+        def softmax_numerators(h, i, exps):
+            channels = slice(P * i, P * (i + 1))
+            logits = []
+            for j in range(HALVES):
+                keys = slice(BANK * j, BANK * (j + 1))
+                bank = psum_logits.tile([P, BANK], F32, tag="logits", name="logits_bank")
+                nc.tensor.matmul_mx(
+                    out=bank[:],
+                    lhsT=q_codes[U_W][:, h, channels].bitcast(FP8X4),
+                    lhsT_scale=q_planes[U_W][:, h, channels],
+                    rhs=q_codes[V_W][:, h, keys].bitcast(FP8X4),
+                    rhs_scale=q_planes[V_W][:, h, keys],
+                    start=True,
+                    stop=True,
+                )
+                logits.append(bank)
+            bank_max = small.tile([P, HALVES], F32)
+            for j in range(HALVES):
+                nc.vector.reduce_max(out=bank_max[:, j : j + 1], in_=logits[j][:], axis=AXIS_X)
+            shift = small.tile([P, 1], F32)
+            nc.vector.tensor_scalar(
+                out=shift[:],
+                in0=bank_max[:, 0:1],
+                scalar1=bank_max[:, 1:2],
+                scalar2=-LOGIT_SCALE,
+                op0=ALU.max,
+                op1=ALU.mult,
+            )
+            for j in range(HALVES):
+                nc.scalar.activation(
+                    out=exps[:, BANK * j : BANK * (j + 1)],
+                    in_=logits[j][:],
+                    func=ACT.Exp,
+                    bias=shift[:],
+                    scale=LOGIT_SCALE,
+                    accum_out=sums[:, i, h, j : j + 1],
+                )
+            twice_sum = small.tile([P, 1], F32)
+            nc.vector.tensor_scalar(
+                out=twice_sum[:],
+                in0=sums[:, i, h, 0:1],
+                scalar1=sums[:, i, h, 1:2],
+                scalar2=2.0,
+                op0=ALU.add,
+                op1=ALU.mult,
+            )
+            weight = small.tile([P, 1], F32)
+            nc.vector.reciprocal(out=weight[:], in_=twice_sum[:])
+            return weight
+
+        for i in range(N_TILES):
+            quantise_x(i)
+
+        for i in range(N_TILES):
+            project(V_W, 0, i, on_scalar=(i % 2 == 0))
+
+        project(U_W, 0, 0, on_scalar=True)
+        for i in range(N_TILES):
+            if i + 1 < N_TILES:
+                project(U_W, 0, i + 1, on_scalar=True)
+            project(V_W, 1, i, on_scalar=False)
+            weight0 = softmax_numerators(0, i, share0[:, i, :])
+            nc.gpsimd.tensor_scalar(
+                out=share0[:, i, :],
+                in0=share0[:, i, :],
+                scalar1=weight0[:],
+                scalar2=0.0,
+                op0=ALU.mult,
+                op1=ALU.add,
+            )
+
+        project(U_W, 1, 0, on_scalar=True)
+        for i in range(N_TILES):
+            if i + 1 < N_TILES:
+                project(U_W, 1, i + 1, on_scalar=True)
+            exps1 = rows.tile([P, C], F32)
+            weight1 = softmax_numerators(1, i, exps1[:])
+            mean = rows.tile([P, C], F32)
+            nc.vector.scalar_tensor_tensor(
+                out=mean[:],
+                in0=exps1[:],
+                scalar=weight1[:],
+                in1=share0[:, i, :],
+                op0=ALU.mult,
+                op1=ALU.add,
+            )
+            result = rows.tile([P, C], F32)
+            nc.vector.tensor_tensor(out=result[:], in0=mean[:], in1=x_sb[:, i, :], op=ALU.mult)
+            nc.sync.dma_start(out=out_dram[P * i : P * (i + 1), :], in_=result[:])

@@ -237,5 +237,5 @@ def tile_dynamicptheadselection_pa_e_kernel(
                 op1=ALU.add,
             )
             result = rows.tile([P, C], F32)
-            nc.vector.tensor_tensor(out=result[:], in0=mean[:], in1=x_sb[:, i, :], op=ALU.mult)
+            nc.gpsimd.tensor_tensor(out=result[:], in0=mean[:], in1=x_sb[:, i, :], op=ALU.mult)
             nc.sync.dma_start(out=out_dram[P * i : P * (i + 1), :], in_=result[:])

@@ -24,9 +24,12 @@ N_TILES = C // P
 G = D // K_PASS
 BANK = 512
 HALVES = C // BANK
+PSUM_BANKS = 8
 U_W = 0
 V_W = 1
 LOGIT_SCALE = 1.0 / math.sqrt(R)
+KEY_BLOCKS_PER_STEP = 2
+LAG = N_TILES // KEY_BLOCKS_PER_STEP
 
 FLOPS = 2 * (2 * C * D * D) + HEADS * 2 * C * C * R
 
@@ -44,9 +47,8 @@ def tile_dynamicptheadselection_pa_e_kernel(
         tc.tile_pool(name="keep", bufs=1) as keep,
         tc.tile_pool(name="stage", bufs=4) as stage,
         tc.tile_pool(name="rows", bufs=3) as rows,
-        tc.tile_pool(name="small", bufs=4) as small,
-        tc.psum_pool(name="psum_work", bufs=4) as psum_work,
-        tc.psum_pool(name="psum_logits", bufs=4) as psum_logits,
+        tc.tile_pool(name="small", bufs=8) as small,
+        tc.psum_pool(name="psum", bufs=PSUM_BANKS) as psum,
     ):
         x_sb = keep.tile([P, N_TILES, D], BF16)
         x_codes = keep.tile([P, N_TILES, G * P], U32, align_bytes=64)
@@ -61,7 +63,7 @@ def tile_dynamicptheadselection_pa_e_kernel(
         q_planes = [
             keep.tile([P, HEADS, C], U8, align_bytes=64, name="q_planes_%d" % w) for w in (U_W, V_W)
         ]
-        share0 = keep.tile([P, N_TILES, C], F32)
+        exps0 = keep.tile([P, N_TILES, C], F32)
         sums = keep.tile([P, N_TILES, HEADS, HALVES], F32)
         identity = keep.tile([P, P], F32)
         warm = keep.tile([P, 1], F32)
@@ -106,7 +108,7 @@ def tile_dynamicptheadselection_pa_e_kernel(
 
         def quantise_x(i):
             x_words = x_sb[:, i, :].bitcast(F32)
-            flipped = psum_work.tile([P, G, 2, P], F32, tag="work")
+            flipped = psum.tile([P, G, 2, P], F32, tag="bank")
             for g in range(G):
                 for u in range(2):
                     nc.tensor.transpose(
@@ -127,7 +129,7 @@ def tile_dynamicptheadselection_pa_e_kernel(
             )
 
         def project(w, h, i, on_scalar):
-            acc = psum_work.tile([P, PACK, P], F32, tag="work")
+            acc = psum.tile([P, PACK, P], F32, tag="bank")
             for t in range(PACK):
                 o_cols = slice(R * h + P * t, R * h + P * (t + 1))
                 for g in range(G):
@@ -155,7 +157,7 @@ def tile_dynamicptheadselection_pa_e_kernel(
             logits = []
             for j in range(HALVES):
                 keys = slice(BANK * j, BANK * (j + 1))
-                bank = psum_logits.tile([P, BANK], F32, tag="logits", name="logits_bank")
+                bank = psum.tile([P, BANK], F32, tag="bank", name="logits_bank")
                 nc.tensor.matmul_mx(
                     out=bank[:],
                     lhsT=q_codes[U_W][:, h, channels].bitcast(FP8X4),
@@ -166,18 +168,20 @@ def tile_dynamicptheadselection_pa_e_kernel(
                     stop=True,
                 )
                 logits.append(bank)
-            bank_max = small.tile([P, HALVES], F32)
+            shift = None
             for j in range(HALVES):
-                nc.vector.reduce_max(out=bank_max[:, j : j + 1], in_=logits[j][:], axis=AXIS_X)
-            shift = small.tile([P, 1], F32)
-            nc.vector.tensor_scalar(
-                out=shift[:],
-                in0=bank_max[:, 0:1],
-                scalar1=bank_max[:, 1:2],
-                scalar2=-LOGIT_SCALE,
-                op0=ALU.max,
-                op1=ALU.mult,
-            )
+                unused = stage.tile([P, BANK], F32)
+                running_min = small.tile([P, 1], F32)
+                nc.vector.tensor_scalar(
+                    out=unused[:],
+                    in0=logits[j][:],
+                    scalar1=-LOGIT_SCALE,
+                    scalar2=(None if shift is None else shift[:]),
+                    op0=ALU.mult,
+                    op1=ALU.min,
+                    accum_out=running_min[:],
+                )
+                shift = running_min
             for j in range(HALVES):
                 nc.scalar.activation(
                     out=exps[:, BANK * j : BANK * (j + 1)],
@@ -187,18 +191,43 @@ def tile_dynamicptheadselection_pa_e_kernel(
                     scale=LOGIT_SCALE,
                     accum_out=sums[:, i, h, j : j + 1],
                 )
-            twice_sum = small.tile([P, 1], F32)
-            nc.vector.tensor_scalar(
-                out=twice_sum[:],
-                in0=sums[:, i, h, 0:1],
-                scalar1=sums[:, i, h, 1:2],
-                scalar2=2.0,
-                op0=ALU.add,
+
+        def combine(i, exps1):
+            twice_sums = small.tile([P, HEADS], F32)
+            for h in range(HEADS):
+                nc.gpsimd.tensor_scalar(
+                    out=twice_sums[:, h : h + 1],
+                    in0=sums[:, i, h, 0:1],
+                    scalar1=sums[:, i, h, 1:2],
+                    scalar2=2.0,
+                    op0=ALU.add,
+                    op1=ALU.mult,
+                )
+            weights = small.tile([P, HEADS], F32)
+            nc.vector.reciprocal(out=weights[:], in_=twice_sums[:])
+            ratio = small.tile([P, 1], F32)
+            nc.gpsimd.tensor_tensor(
+                out=ratio[:], in0=twice_sums[:, 1:2], in1=weights[:, 0:1], op=ALU.mult
+            )
+            mixed = rows.tile([P, C], F32)
+            nc.vector.scalar_tensor_tensor(
+                out=mixed[:],
+                in0=exps0[:, i, :],
+                scalar=ratio[:],
+                in1=exps1[:],
+                op0=ALU.mult,
+                op1=ALU.add,
+            )
+            result = rows.tile([P, C], F32)
+            nc.vector.scalar_tensor_tensor(
+                out=result[:],
+                in0=mixed[:],
+                scalar=weights[:, 1:2],
+                in1=x_sb[:, i, :],
+                op0=ALU.mult,
                 op1=ALU.mult,
             )
-            weight = small.tile([P, 1], F32)
-            nc.vector.reciprocal(out=weight[:], in_=twice_sum[:])
-            return weight
+            nc.sync.dma_start(out=out_dram[P * i : P * (i + 1), :], in_=result[:])
 
         for i in range(N_TILES):
             quantise_x(i)
@@ -207,35 +236,22 @@ def tile_dynamicptheadselection_pa_e_kernel(
             project(V_W, 0, i, on_scalar=(i % 2 == 0))
 
         project(U_W, 0, 0, on_scalar=True)
-        for i in range(N_TILES):
-            if i + 1 < N_TILES:
-                project(U_W, 0, i + 1, on_scalar=True)
-            project(V_W, 1, i, on_scalar=False)
-            weight0 = softmax_numerators(0, i, share0[:, i, :])
-            nc.gpsimd.tensor_scalar(
-                out=share0[:, i, :],
-                in0=share0[:, i, :],
-                scalar1=weight0[:],
-                scalar2=0.0,
-                op0=ALU.mult,
-                op1=ALU.add,
-            )
-
-        project(U_W, 1, 0, on_scalar=True)
-        for i in range(N_TILES):
-            if i + 1 < N_TILES:
-                project(U_W, 1, i + 1, on_scalar=True)
-            exps1 = rows.tile([P, C], F32)
-            weight1 = softmax_numerators(1, i, exps1[:])
-            mean = rows.tile([P, C], F32)
-            nc.vector.scalar_tensor_tensor(
-                out=mean[:],
-                in0=exps1[:],
-                scalar=weight1[:],
-                in1=share0[:, i, :],
-                op0=ALU.mult,
-                op1=ALU.add,
-            )
-            result = rows.tile([P, C], F32)
-            nc.gpsimd.tensor_tensor(out=result[:], in0=mean[:], in1=x_sb[:, i, :], op=ALU.mult)
-            nc.sync.dma_start(out=out_dram[P * i : P * (i + 1), :], in_=result[:])
+        exps1_of_tile = {}
+        for step in range(N_TILES + LAG + 1):
+            tile0 = step
+            tile1 = step - LAG
+            if tile0 + 1 < N_TILES:
+                project(U_W, 0, tile0 + 1, on_scalar=True)
+            if step < LAG:
+                for block in range(KEY_BLOCKS_PER_STEP * step, KEY_BLOCKS_PER_STEP * (step + 1)):
+                    project(V_W, 1, block, on_scalar=(block % 2 == 0))
+            if 0 <= tile1 + 1 < N_TILES:
+                project(U_W, 1, tile1 + 1, on_scalar=True)
+            if tile0 < N_TILES:
+                softmax_numerators(0, tile0, exps0[:, tile0, :])
+            if 0 <= tile1 < N_TILES:
+                exps1 = rows.tile([P, C], F32)
+                softmax_numerators(1, tile1, exps1[:])
+                exps1_of_tile[tile1] = exps1
+            if tile1 - 1 >= 0:
+                combine(tile1 - 1, exps1_of_tile[tile1 - 1])

@@ -30,6 +30,7 @@ V_W = 1
 LOGIT_SCALE = 1.0 / math.sqrt(R)
 KEY_BLOCKS_PER_STEP = 2
 LAG = N_TILES // KEY_BLOCKS_PER_STEP
+ROUNDED_MAX_UNITS = tuple((1, i) for i in range(N_TILES - LAG, N_TILES))
 
 FLOPS = 2 * (2 * C * D * D) + HEADS * 2 * C * C * R
 
@@ -48,6 +49,7 @@ def tile_dynamicptheadselection_pa_e_kernel(
         tc.tile_pool(name="stage", bufs=4) as stage,
         tc.tile_pool(name="rows", bufs=3) as rows,
         tc.tile_pool(name="small", bufs=8) as small,
+        tc.tile_pool(name="lowp", bufs=3) as lowp,
         tc.psum_pool(name="psum", bufs=PSUM_BANKS) as psum,
     ):
         x_sb = keep.tile([P, N_TILES, D], BF16)
@@ -168,20 +170,41 @@ def tile_dynamicptheadselection_pa_e_kernel(
                     stop=True,
                 )
                 logits.append(bank)
-            shift = None
-            for j in range(HALVES):
-                unused = stage.tile([P, BANK], F32)
-                running_min = small.tile([P, 1], F32)
+            if (h, i) in ROUNDED_MAX_UNITS:
+                rounded = lowp.tile([P, C], BF16)
+                for j in range(HALVES):
+                    nc.scalar.activation(
+                        out=rounded[:, BANK * j : BANK * (j + 1)],
+                        in_=logits[j][:],
+                        func=ACT.Copy,
+                        scale=-LOGIT_SCALE,
+                    )
+                unused_row = lowp.tile([P, C], BF16)
+                shift = small.tile([P, 1], F32, name="rounded_shift")
                 nc.vector.tensor_scalar(
-                    out=unused[:],
-                    in0=logits[j][:],
-                    scalar1=-LOGIT_SCALE,
-                    scalar2=(None if shift is None else shift[:]),
+                    out=unused_row[:],
+                    in0=rounded[:],
+                    scalar1=1.0,
+                    scalar2=None,
                     op0=ALU.mult,
                     op1=ALU.min,
-                    accum_out=running_min[:],
+                    accum_out=shift[:],
                 )
-                shift = running_min
+            else:
+                shift = None
+                for j in range(HALVES):
+                    unused = stage.tile([P, BANK], F32)
+                    running_min = small.tile([P, 1], F32)
+                    nc.vector.tensor_scalar(
+                        out=unused[:],
+                        in0=logits[j][:],
+                        scalar1=-LOGIT_SCALE,
+                        scalar2=(None if shift is None else shift[:]),
+                        op0=ALU.mult,
+                        op1=ALU.min,
+                        accum_out=running_min[:],
+                    )
+                    shift = running_min
             for j in range(HALVES):
                 nc.scalar.activation(
                     out=exps[:, BANK * j : BANK * (j + 1)],

@@ -50,6 +50,7 @@ def tile_dynamicptheadselection_pa_e_kernel(
         tc.tile_pool(name="rows", bufs=3) as rows,
         tc.tile_pool(name="small", bufs=8) as small,
         tc.tile_pool(name="lowp", bufs=3) as lowp,
+        tc.tile_pool(name="moved", bufs=4) as moved,
         tc.psum_pool(name="psum", bufs=PSUM_BANKS) as psum,
     ):
         x_sb = keep.tile([P, N_TILES, D], BF16)
@@ -72,6 +73,7 @@ def tile_dynamicptheadselection_pa_e_kernel(
 
         nc.vector.memset(w_planes[:].bitcast(I32), 0)
         nc.vector.memset(warm[:], 0.0)
+        nc.vector.memset(sums[:], 0.0)
         nc.scalar.activation(out=warm[:], in_=warm[:], func=ACT.Exp)
         make_identity(nc, identity[:])
 
@@ -190,13 +192,22 @@ def tile_dynamicptheadselection_pa_e_kernel(
                     op1=ALU.min,
                     accum_out=shift[:],
                 )
+                for j in range(HALVES):
+                    nc.scalar.activation(
+                        out=exps[:, BANK * j : BANK * (j + 1)],
+                        in_=logits[j][:],
+                        func=ACT.Exp,
+                        bias=shift[:],
+                        scale=LOGIT_SCALE,
+                        accum_out=sums[:, i, h, j : j + 1],
+                    )
             else:
+                negated = moved.tile([P, C], F32)
                 shift = None
                 for j in range(HALVES):
-                    unused = stage.tile([P, BANK], F32)
                     running_min = small.tile([P, 1], F32)
                     nc.vector.tensor_scalar(
-                        out=unused[:],
+                        out=negated[:, BANK * j : BANK * (j + 1)],
                         in0=logits[j][:],
                         scalar1=-LOGIT_SCALE,
                         scalar2=(None if shift is None else shift[:]),
@@ -205,14 +216,13 @@ def tile_dynamicptheadselection_pa_e_kernel(
                         accum_out=running_min[:],
                     )
                     shift = running_min
-            for j in range(HALVES):
                 nc.scalar.activation(
-                    out=exps[:, BANK * j : BANK * (j + 1)],
-                    in_=logits[j][:],
+                    out=exps,
+                    in_=negated[:],
                     func=ACT.Exp,
                     bias=shift[:],
-                    scale=LOGIT_SCALE,
-                    accum_out=sums[:, i, h, j : j + 1],
+                    scale=-1.0,
+                    accum_out=sums[:, i, h, 0:1],
                 )
 
         def combine(i, exps1):

@@ -68,6 +68,7 @@ def tile_dynamicptheadselection_pa_e_kernel(
         ]
         exps0 = keep.tile([P, N_TILES, C], F32)
         sums = keep.tile([P, N_TILES, HEADS, HALVES], F32)
+        inverse_sums0 = keep.tile([P, N_TILES], F32)
         identity = keep.tile([P, P], F32)
         warm = keep.tile([P, 1], F32)
 
@@ -225,22 +226,30 @@ def tile_dynamicptheadselection_pa_e_kernel(
                     accum_out=sums[:, i, h, 0:1],
                 )
 
+        def invert_head0_sums(first, count):
+            nc.vector.reciprocal(
+                out=inverse_sums0[:, first : first + count],
+                in_=sums[:, first : first + count, 0, 0],
+            )
+
         def combine(i, exps1):
-            twice_sums = small.tile([P, HEADS], F32)
-            for h in range(HEADS):
-                nc.gpsimd.tensor_scalar(
-                    out=twice_sums[:, h : h + 1],
-                    in0=sums[:, i, h, 0:1],
-                    scalar1=sums[:, i, h, 1:2],
-                    scalar2=2.0,
-                    op0=ALU.add,
-                    op1=ALU.mult,
-                )
-            weights = small.tile([P, HEADS], F32)
-            nc.vector.reciprocal(out=weights[:], in_=twice_sums[:])
             ratio = small.tile([P, 1], F32)
-            nc.gpsimd.tensor_tensor(
-                out=ratio[:], in0=twice_sums[:, 1:2], in1=weights[:, 0:1], op=ALU.mult
+            nc.gpsimd.tensor_scalar(
+                out=ratio[:],
+                in0=sums[:, i, 1, 0:1],
+                scalar1=sums[:, i, 1, 1:2],
+                scalar2=inverse_sums0[:, i : i + 1],
+                op0=ALU.add,
+                op1=ALU.mult,
+            )
+            twice_sum1 = small.tile([P, 1], F32)
+            nc.gpsimd.tensor_scalar(
+                out=twice_sum1[:],
+                in0=sums[:, i, 1, 0:1],
+                scalar1=sums[:, i, 1, 1:2],
+                scalar2=2.0,
+                op0=ALU.add,
+                op1=ALU.mult,
             )
             mixed = rows.tile([P, C], F32)
             nc.vector.scalar_tensor_tensor(
@@ -251,11 +260,13 @@ def tile_dynamicptheadselection_pa_e_kernel(
                 op0=ALU.mult,
                 op1=ALU.add,
             )
+            weight1 = small.tile([P, 1], F32)
+            nc.vector.reciprocal(out=weight1[:], in_=twice_sum1[:])
             result = rows.tile([P, C], F32)
             nc.vector.scalar_tensor_tensor(
                 out=result[:],
                 in0=mixed[:],
-                scalar=weights[:, 1:2],
+                scalar=weight1[:],
                 in1=x_sb[:, i, :],
                 op0=ALU.mult,
                 op1=ALU.mult,
@@ -286,5 +297,9 @@ def tile_dynamicptheadselection_pa_e_kernel(
                 exps1 = rows.tile([P, C], F32)
                 softmax_numerators(1, tile1, exps1[:])
                 exps1_of_tile[tile1] = exps1
+            if step == LAG:
+                invert_head0_sums(0, LAG)
+            if step == N_TILES:
+                invert_head0_sums(LAG, N_TILES - LAG)
             if tile1 - 1 >= 0:
                 combine(tile1 - 1, exps1_of_tile[tile1 - 1])

@@ -289,8 +289,10 @@ def tile_dynamicptheadselection_pa_e_kernel(
             if step < LAG:
                 for block in range(KEY_BLOCKS_PER_STEP * step, KEY_BLOCKS_PER_STEP * (step + 1)):
                     project(V_W, 1, block, on_scalar=(block % 2 == 0))
-            if 0 <= tile1 + 1 < N_TILES:
+            if 0 <= tile1 + 1 and step < N_TILES:
                 project(U_W, 1, tile1 + 1, on_scalar=True)
+            if N_TILES - LAG < step < N_TILES:
+                project(U_W, 1, step, on_scalar=True)
             if tile0 < N_TILES:
                 softmax_numerators(0, tile0, exps0[:, tile0, :])
             if 0 <= tile1 < N_TILES:

@@ -30,6 +30,7 @@ V_W = 1
 LOGIT_SCALE = 1.0 / math.sqrt(R)
 KEY_BLOCKS_PER_STEP = 2
 LAG = N_TILES // KEY_BLOCKS_PER_STEP
+VECTOR_COPIED_KEY_BLOCKS = (1, 3, 5)
 ROUNDED_MAX_UNITS = tuple((1, i) for i in range(N_TILES - LAG, N_TILES))
 
 FLOPS = 2 * (2 * C * D * D) + HEADS * 2 * C * C * R
@@ -288,7 +289,7 @@ def tile_dynamicptheadselection_pa_e_kernel(
                 project(U_W, 0, tile0 + 1, on_scalar=True)
             if step < LAG:
                 for block in range(KEY_BLOCKS_PER_STEP * step, KEY_BLOCKS_PER_STEP * (step + 1)):
-                    project(V_W, 1, block, on_scalar=(block % 2 == 0))
+                    project(V_W, 1, block, on_scalar=(block not in VECTOR_COPIED_KEY_BLOCKS))
             if 0 <= tile1 + 1 and step < N_TILES:
                 project(U_W, 1, tile1 + 1, on_scalar=True)
             if N_TILES - LAG < step < N_TILES:

import math

import concourse.mybir as mybir
from concourse.masks import make_identity

F32 = mybir.dt.float32
BF16 = mybir.dt.bfloat16
I32 = mybir.dt.int32
U32 = mybir.dt.uint32
U8 = mybir.dt.uint8
FP8X4 = mybir.dt.float8_e4m3fn_x4
ALU = mybir.AluOpType
ACT = mybir.ActivationFunctionType
AXIS_X = mybir.AxisListType.X

P = 128
PACK = 4
K_PASS = P * PACK
C = 1024
D = 1024
HEADS = 2
R = D // HEADS
N_TILES = C // P
G = D // K_PASS
BANK = 512
HALVES = C // BANK
PSUM_BANKS = 8
U_W = 0
V_W = 1
LOGIT_SCALE = 1.0 / math.sqrt(R)
KEY_BLOCKS_PER_STEP = 2
LAG = N_TILES // KEY_BLOCKS_PER_STEP
VECTOR_COPIED_KEY_BLOCKS = (1, 3, 5)
ROUNDED_MAX_UNITS = tuple((1, i) for i in range(N_TILES - LAG, N_TILES))

FLOPS = 2 * (2 * C * D * D) + HEADS * 2 * C * C * R


def tile_dynamicptheadselection_pa_e_kernel(
    tc, qz, u_words, u_scales, v_words, v_scales, out
):
    nc = tc.nc
    x_dram = qz.rearrange("b c q d -> (b c q) d")
    out_dram = out.rearrange("b c q d -> (b c q) d")
    w_words_dram = [u_words, v_words]
    w_scales_dram = [u_scales, v_scales]

    with (
        tc.tile_pool(name="keep", bufs=1) as keep,
        tc.tile_pool(name="stage", bufs=4) as stage,
        tc.tile_pool(name="rows", bufs=3) as rows,
        tc.tile_pool(name="small", bufs=8) as small,
        tc.tile_pool(name="lowp", bufs=3) as lowp,
        tc.tile_pool(name="moved", bufs=4) as moved,
        tc.psum_pool(name="psum", bufs=PSUM_BANKS) as psum,
    ):
        x_sb = keep.tile([P, N_TILES, D], BF16)
        x_codes = keep.tile([P, N_TILES, G * P], U32, align_bytes=64)
        x_planes = keep.tile([P, N_TILES, G * P], U8, align_bytes=64)
        w_codes = [
            keep.tile([P, G, D], U32, align_bytes=64, name="w_codes_%d" % w) for w in (U_W, V_W)
        ]
        w_planes = keep.tile([P, D], U8, align_bytes=64)
        q_codes = [
            keep.tile([P, HEADS, C], U32, align_bytes=64, name="q_codes_%d" % w) for w in (U_W, V_W)
        ]
        q_planes = [
            keep.tile([P, HEADS, C], U8, align_bytes=64, name="q_planes_%d" % w) for w in (U_W, V_W)
        ]
        exps0 = keep.tile([P, N_TILES, C], F32)
        sums = keep.tile([P, N_TILES, HEADS, HALVES], F32)
        inverse_sums0 = keep.tile([P, N_TILES], F32)
        identity = keep.tile([P, P], F32)
        warm = keep.tile([P, 1], F32)

        nc.vector.memset(w_planes[:].bitcast(I32), 0)
        nc.vector.memset(warm[:], 0.0)
        nc.vector.memset(sums[:], 0.0)
        nc.scalar.activation(out=warm[:], in_=warm[:], func=ACT.Exp)
        make_identity(nc, identity[:])

        def load_weight_codes(w, h):
            cols = w_words_dram[w].rearrange("g p n t -> p g (n t)")
            nc.sync.dma_start(
                out=w_codes[w][:, :, R * h : R * (h + 1)].bitcast(I32),
                in_=cols[:, :, PACK * R * h : PACK * R * (h + 1)].bitcast(I32),
            )

        def load_weight_scales(w):
            for quadrant in range(4):
                first = 32 * quadrant + PACK * G * w
                nc.sync.dma_start(
                    out=w_planes[first : first + PACK * G, :].bitcast(I32),
                    in_=w_scales_dram[w][:, PACK * quadrant : PACK * (quadrant + 1), :].bitcast(I32),
                )

        for pair in range(N_TILES // 2):
            nc.sync.dma_start(
                out=x_sb[:, 2 * pair : 2 * pair + 2, :],
                in_=x_dram[2 * P * pair : 2 * P * (pair + 1), :].rearrange("(i p) d -> p i d", p=P),
            )
        load_weight_scales(V_W)
        load_weight_codes(V_W, 0)
        load_weight_codes(U_W, 0)
        load_weight_scales(U_W)
        load_weight_codes(V_W, 1)
        load_weight_codes(U_W, 1)

        def copy_out(engine_is_scalar, dst, src):
            if engine_is_scalar:
                nc.scalar.copy(out=dst, in_=src)
            else:
                nc.vector.tensor_copy(out=dst, in_=src)

        def quantise_x(i):
            x_words = x_sb[:, i, :].bitcast(F32)
            flipped = psum.tile([P, G, 2, P], F32, tag="bank")
            for g in range(G):
                for u in range(2):
                    nc.tensor.transpose(
                        flipped[:, g, u, :],
                        x_words[:, (K_PASS // 2) * g + u : (K_PASS // 2) * (g + 1) : 2],
                        identity[:],
                    )
            x_grouped = stage.tile([P, G, P, PACK], BF16, align_bytes=64)
            copy_out(
                i % 2 == 0,
                x_grouped[:].bitcast(F32),
                flipped[:].rearrange("p g u c -> p g c u"),
            )
            nc.vector.quantize_mx(
                out=x_codes[:, i, :].bitcast(FP8X4),
                scales=x_planes[:, i, :],
                in_=x_grouped[:].rearrange("p g c t -> p (g c t)"),
            )

        def project(w, h, i, on_scalar):
            acc = psum.tile([P, PACK, P], F32, tag="bank")
            for t in range(PACK):
                o_cols = slice(R * h + P * t, R * h + P * (t + 1))
                for g in range(G):
                    c_cols = slice(P * g, P * (g + 1))
                    nc.tensor.matmul_mx(
                        out=acc[:, t, :],
                        lhsT=w_codes[w][:, g, o_cols].bitcast(FP8X4),
                        lhsT_scale=w_planes[PACK * (G * w + g) : P, o_cols],
                        rhs=x_codes[:, i, c_cols].bitcast(FP8X4),
                        rhs_scale=x_planes[:, i, c_cols],
                        start=(g == 0),
                        stop=(g == G - 1),
                    )
            grouped = stage.tile([P, P, PACK], BF16, align_bytes=64)
            copy_out(on_scalar, grouped[:], acc[:].rearrange("p t c -> p c t"))
            channels = slice(P * i, P * (i + 1))
            nc.vector.quantize_mx(
                out=q_codes[w][:, h, channels].bitcast(FP8X4),
                scales=q_planes[w][:, h, channels],
                in_=grouped[:].rearrange("p c t -> p (c t)"),
            )

        def softmax_numerators(h, i, exps):
            channels = slice(P * i, P * (i + 1))
            logits = []
            for j in range(HALVES):
                keys = slice(BANK * j, BANK * (j + 1))
                bank = psum.tile([P, BANK], F32, tag="bank", name="logits_bank")
                nc.tensor.matmul_mx(
                    out=bank[:],
                    lhsT=q_codes[U_W][:, h, channels].bitcast(FP8X4),
                    lhsT_scale=q_planes[U_W][:, h, channels],
                    rhs=q_codes[V_W][:, h, keys].bitcast(FP8X4),
                    rhs_scale=q_planes[V_W][:, h, keys],
                    start=True,
                    stop=True,
                )
                logits.append(bank)
            if (h, i) in ROUNDED_MAX_UNITS:
                rounded = lowp.tile([P, C], BF16)
                for j in range(HALVES):
                    nc.scalar.activation(
                        out=rounded[:, BANK * j : BANK * (j + 1)],
                        in_=logits[j][:],
                        func=ACT.Copy,
                        scale=-LOGIT_SCALE,
                    )
                unused_row = lowp.tile([P, C], BF16)
                shift = small.tile([P, 1], F32, name="rounded_shift")
                nc.vector.tensor_scalar(
                    out=unused_row[:],
                    in0=rounded[:],
                    scalar1=1.0,
                    scalar2=None,
                    op0=ALU.mult,
                    op1=ALU.min,
                    accum_out=shift[:],
                )
                for j in range(HALVES):
                    nc.scalar.activation(
                        out=exps[:, BANK * j : BANK * (j + 1)],
                        in_=logits[j][:],
                        func=ACT.Exp,
                        bias=shift[:],
                        scale=LOGIT_SCALE,
                        accum_out=sums[:, i, h, j : j + 1],
                    )
            else:
                negated = moved.tile([P, C], F32)
                shift = None
                for j in range(HALVES):
                    running_min = small.tile([P, 1], F32)
                    nc.vector.tensor_scalar(
                        out=negated[:, BANK * j : BANK * (j + 1)],
                        in0=logits[j][:],
                        scalar1=-LOGIT_SCALE,
                        scalar2=(None if shift is None else shift[:]),
                        op0=ALU.mult,
                        op1=ALU.min,
                        accum_out=running_min[:],
                    )
                    shift = running_min
                nc.scalar.activation(
                    out=exps,
                    in_=negated[:],
                    func=ACT.Exp,
                    bias=shift[:],
                    scale=-1.0,
                    accum_out=sums[:, i, h, 0:1],
                )

        def invert_head0_sums(first, count):
            nc.vector.reciprocal(
                out=inverse_sums0[:, first : first + count],
                in_=sums[:, first : first + count, 0, 0],
            )

        def combine(i, exps1):
            ratio = small.tile([P, 1], F32)
            nc.gpsimd.tensor_scalar(
                out=ratio[:],
                in0=sums[:, i, 1, 0:1],
                scalar1=sums[:, i, 1, 1:2],
                scalar2=inverse_sums0[:, i : i + 1],
                op0=ALU.add,
                op1=ALU.mult,
            )
            twice_sum1 = small.tile([P, 1], F32)
            nc.gpsimd.tensor_scalar(
                out=twice_sum1[:],
                in0=sums[:, i, 1, 0:1],
                scalar1=sums[:, i, 1, 1:2],
                scalar2=2.0,
                op0=ALU.add,
                op1=ALU.mult,
            )
            mixed = rows.tile([P, C], F32)
            nc.vector.scalar_tensor_tensor(
                out=mixed[:],
                in0=exps0[:, i, :],
                scalar=ratio[:],
                in1=exps1[:],
                op0=ALU.mult,
                op1=ALU.add,
            )
            weight1 = small.tile([P, 1], F32)
            nc.vector.reciprocal(out=weight1[:], in_=twice_sum1[:])
            result = rows.tile([P, C], F32)
            nc.vector.scalar_tensor_tensor(
                out=result[:],
                in0=mixed[:],
                scalar=weight1[:],
                in1=x_sb[:, i, :],
                op0=ALU.mult,
                op1=ALU.mult,
            )
            nc.sync.dma_start(out=out_dram[P * i : P * (i + 1), :], in_=result[:])

        for i in range(N_TILES):
            quantise_x(i)

        for i in range(N_TILES):
            project(V_W, 0, i, on_scalar=(i % 2 == 0))

        project(U_W, 0, 0, on_scalar=True)
        exps1_of_tile = {}
        for step in range(N_TILES + LAG + 1):
            tile0 = step
            tile1 = step - LAG
            if tile0 + 1 < N_TILES:
                project(U_W, 0, tile0 + 1, on_scalar=True)
            if step < LAG:
                for block in range(KEY_BLOCKS_PER_STEP * step, KEY_BLOCKS_PER_STEP * (step + 1)):
                    project(V_W, 1, block, on_scalar=(block not in VECTOR_COPIED_KEY_BLOCKS))
            if 0 <= tile1 + 1 and step < N_TILES:
                project(U_W, 1, tile1 + 1, on_scalar=True)
            if N_TILES - LAG < step < N_TILES:
                project(U_W, 1, step, on_scalar=True)
            if tile0 < N_TILES:
                softmax_numerators(0, tile0, exps0[:, tile0, :])
            if 0 <= tile1 < N_TILES:
                exps1 = rows.tile([P, C], F32)
                softmax_numerators(1, tile1, exps1[:])
                exps1_of_tile[tile1] = exps1
            if step == LAG:
                invert_head0_sums(0, LAG)
            if step == N_TILES:
                invert_head0_sums(LAG, N_TILES - LAG)
            if tile1 - 1 >= 0:
                combine(tile1 - 1, exps1_of_tile[tile1 - 1])
